import numpy as np
import ml_dtypes


def mxq(x, axis, fmt="e4m3"):
    dtype, down = {"e4m3": (ml_dtypes.float8_e4m3fn, 7), "e5m2": (ml_dtypes.float8_e5m2, 14)}[fmt]
    v = np.moveaxis(np.asarray(x, np.float32).astype(ml_dtypes.bfloat16).astype(np.float64), axis, -1)
    blocks = v.reshape(v.shape[:-1] + (-1, 32))
    amax = np.abs(blocks).max(-1, keepdims=True)
    byte = np.maximum(np.where(amax > 0, np.frexp(amax)[1] - 1 + 127, 0) - down, 1)
    scale = np.exp2(byte - 127.0)
    codes = (blocks / scale).astype(np.float32).astype(dtype).astype(np.float64)
    return np.moveaxis((codes * scale).reshape(v.shape), -1, axis)


WIDE = False


def mx_kscale(k):
    if not WIDE:
        return np.ones(k)
    levels = np.array([10, -10, 5, -5, 0])
    a = np.random.permutation(np.resize(levels, k // 512 * 4)).reshape(k // 512, 4)
    idx = np.arange(k)
    return np.exp2(a[idx // 512, idx % 128 // 32])


BF16 = ml_dtypes.bfloat16


def bf(x):
    return np.asarray(x, np.float32).astype(BF16)


def f64(x):
    return np.asarray(x).astype(np.float64)


B, S, H, NH = 4, 256, 1024, 16
LN_EPS = 1e-5


def silu(v):
    return v / (1.0 + np.exp(-v))


def setup_inputs():
    s, t = mx_kscale(H), mx_kscale(H)
    w = 1.0 / np.sqrt(H)
    z = (np.random.standard_normal((B, S, H)) + 0.3 * np.random.standard_normal((B, S, 1))) * 2.0 / S
    return {"z": bf(z),
            "hidden_states": bf(np.random.standard_normal((B, S, H)) * s),
            "Wg": bf(np.random.standard_normal((H, H)) * w / s[:, None]),
            "Wo": bf(np.random.standard_normal((H, H)) * w / t[:, None]),
            "gamma": bf((1.0 + 0.1 * np.random.standard_normal(H)) * t),
            "beta": bf(0.1 * np.random.standard_normal(H) * t)}


def reference(z, hidden_states, Wg, Wo, gamma, beta):
    z = f64(z)
    g = mxq(f64(hidden_states), 2, "e4m3") @ mxq(f64(Wg), 0, "e4m3")
    mu = np.mean(z, axis=-1, keepdims=True)
    var = np.mean(np.square(z - mu), axis=-1, keepdims=True)
    zn = (z - mu) * (1.0 / np.sqrt(var + LN_EPS)) * f64(gamma) + f64(beta)
    h = zn * silu(g)
    return mxq(h, 2, "e4m3") @ mxq(f64(Wo), 0, "e4m3")

@@ -1,0 +1,297 @@
+from contextlib import ExitStack
+
+import concourse.mybir as mybir
+from concourse.masks import make_identity
+
+F32 = mybir.dt.float32
+BF16 = mybir.dt.bfloat16
+U32 = mybir.dt.uint32
+U8 = mybir.dt.uint8
+FP8X4 = mybir.dt.float8_e4m3fn_x4
+ALU = mybir.AluOpType
+ACT = mybir.ActivationFunctionType
+
+P = 128
+PACK = 4
+K_PASS = P * PACK
+TOKENS = 1024
+H = 1024
+PASSES = H // K_PASS
+TOKEN_TILES = TOKENS // P
+FEATURE_TILES = H // P
+CHUNK_TILES = 2
+CHUNK = CHUNK_TILES * P
+CHUNKS = TOKENS // CHUNK
+N_OUT = 512
+LN_EPS = 1e-5
+W_PIECE = 512
+BN_WIDTH = 512
+
+FLOPS = 2 * 2 * TOKENS * H * H
+
+
+def tile_gatedlinearattention_pb_kernel(tc, z, hidden_states, Wg, Wo, gamma, beta, out):
+    nc = tc.nc
+    x_dram = hidden_states.flatten_outer_dims()
+    z_dram = z.flatten_outer_dims()
+    out_dram = out.flatten_outer_dims()
+
+    with ExitStack() as ctx:
+        ctx.enter_context(tc.manual_schedule())
+        keep = ctx.enter_context(tc.tile_pool(name="keep", bufs=1))
+        stage = ctx.enter_context(tc.tile_pool(name="stage", bufs=3))
+        small = ctx.enter_context(tc.tile_pool(name="small", bufs=TOKEN_TILES))
+        normed = ctx.enter_context(tc.tile_pool(name="normed", bufs=2 * CHUNK_TILES))
+        units = ctx.enter_context(tc.tile_pool(name="units", bufs=CHUNKS * PASSES))
+        result = ctx.enter_context(tc.tile_pool(name="result", bufs=6))
+        psum = ctx.enter_context(tc.psum_pool(name="psum", bufs=8))
+
+        def chunk_tiles(ch):
+            return range(ch * CHUNK_TILES, (ch + 1) * CHUNK_TILES)
+
+        z_all = keep.tile([P, TOKEN_TILES, H], BF16)
+        x_all = keep.tile([P, TOKEN_TILES * H], BF16)
+        wg_raw = keep.tile([P, PASSES, PACK, H], BF16)
+        wo_raw = keep.tile([P, PASSES, PACK, H], BF16)
+
+        def load_z(ch):
+            first = ch * CHUNK_TILES
+            nc.sync.dma_start(
+                out=z_all[:, first : first + CHUNK_TILES, :],
+                in_=z_dram[ch * CHUNK : (ch + 1) * CHUNK, :].rearrange("(t p) k -> p t k", p=P),
+            )
+
+        def load_x(ch):
+            nc.sync.dma_start(
+                out=x_all[:, ch * CHUNK_TILES * H : (ch + 1) * CHUNK_TILES * H].rearrange("p (t k) -> p t k", k=H),
+                in_=x_dram[ch * CHUNK : (ch + 1) * CHUNK, :].rearrange("(t p) k -> p t k", p=P),
+            )
+
+        gb_rows = keep.tile([P, P], BF16)
+        nc.gpsimd.memset(gb_rows[:], 0.0)
+
+        load_z(0)
+        nc.sync.dma_start(out=gb_rows[0:FEATURE_TILES, :], in_=gamma.rearrange("(f p) -> f p", p=P))
+        nc.sync.dma_start(
+            out=gb_rows[FEATURE_TILES : 2 * FEATURE_TILES, :], in_=beta.rearrange("(f p) -> f p", p=P)
+        )
+        load_x(0)
+        for ch in range(1, CHUNKS):
+            load_z(ch)
+            load_x(ch)
+        for c in range(PASSES):
+            nc.sync.dma_start(
+                out=wg_raw[:, c].rearrange("q (u e) n -> q u e n", u=2),
+                in_=Wg[c * K_PASS : (c + 1) * K_PASS, :].rearrange("(u q e) n -> q u e n", u=2, e=2),
+            )
+        for c in range(PASSES):
+            nc.sync.dma_start(
+                out=wo_raw[:, c],
+                in_=Wo[c * K_PASS : (c + 1) * K_PASS, :].rearrange("(j p) m -> p j m", p=P),
+            )
+
+        neg_half = keep.tile([P, 1], F32)
+        nc.gpsimd.memset(neg_half[:], -0.5)
+        ident_f32 = keep.tile([P, P], F32)
+        make_identity(nc, ident_f32[:])
+        ident_bf16 = keep.tile([P, P], BF16)
+        make_identity(nc, ident_bf16[:])
+        gb_col = keep.tile([P, 2 * FEATURE_TILES], F32)
+
+        def spread_gamma_beta():
+            gb_t = psum.tile([P, P], BF16, tag="bank")
+            nc.tensor.transpose(gb_t[:], gb_rows[:], ident_bf16[:])
+            nc.vector.tensor_copy(out=gb_col[:], in_=gb_t[:, 0 : 2 * FEATURE_TILES])
+
+        wg_codes = keep.tile([P, PASSES, H], U32, align_bytes=64)
+        wg_scales = keep.tile([P, PASSES, H], U8, align_bytes=64)
+        wo_codes = keep.tile([P, PASSES, H], U32, align_bytes=64)
+        wo_scales = keep.tile([P, PASSES, H], U8, align_bytes=64)
+        x_codes = keep.tile([P, PASSES, TOKENS], U32, align_bytes=64)
+        x_scales = keep.tile([P, PASSES, TOKENS], U8, align_bytes=64)
+        h_codes = keep.tile([P, PASSES, TOKENS], U32, align_bytes=64)
+        h_scales = keep.tile([P, PASSES, TOKENS], U8, align_bytes=64)
+
+        def quantise_piece(piece, codes, scales):
+            grouped, c, cols = piece
+            nc.vector.quantize_mx(
+                out=codes[:, c, cols].bitcast(FP8X4),
+                scales=scales[:, c, cols],
+                in_=grouped[:].rearrange("p n j -> p (n j)"),
+            )
+
+        def quantise_weight(raw, codes, scales):
+            waiting = None
+            for c in range(PASSES):
+                for first in range(0, H, W_PIECE):
+                    cols = slice(first, first + W_PIECE)
+                    grouped = stage.tile([P, W_PIECE, PACK], BF16, align_bytes=64)
+                    nc.vector.tensor_copy(
+                        out=grouped[:].rearrange("p (a i) j -> p a j i", i=4),
+                        in_=raw[:, c, :, cols].rearrange("p j (a i) -> p a j i", i=4),
+                    )
+                    if waiting is not None:
+                        quantise_piece(waiting, codes, scales)
+                    waiting = (grouped, c, cols)
+            quantise_piece(waiting, codes, scales)
+
+        x_words = x_all[:].bitcast(F32)
+        words_per_tile = H // 2
+        x_grouped = {}
+
+        def transpose_x(ch):
+            grouped = stage.tile([P, PASSES * CHUNK * PACK], BF16, align_bytes=64, name="x_grouped")
+            grouped_words = grouped[:].bitcast(F32).rearrange("p (c t u) -> p c t u", c=PASSES, u=2)
+            for tl, tt in enumerate(chunk_tiles(ch)):
+                xt = psum.tile([P, 2 * PASSES, P], F32, tag="bank")
+                for b in range(2 * PASSES):
+                    first = tt * words_per_tile + b * P
+                    nc.tensor.transpose(xt[:, b, :], x_words[:, first : first + P], ident_f32[:])
+                nc.scalar.copy(
+                    out=grouped_words[:, :, tl * P : (tl + 1) * P, :],
+                    in_=xt[:].rearrange("p (c u) t -> p c t u", u=2),
+                )
+            x_grouped[ch] = grouped
+
+        def quantise_x(ch):
+            toks = slice(ch * CHUNK, (ch + 1) * CHUNK)
+            for c in range(PASSES):
+                nc.vector.quantize_mx(
+                    out=x_codes[:, c, toks].bitcast(FP8X4),
+                    scales=x_scales[:, c, toks],
+                    in_=x_grouped[ch][:, c * CHUNK * PACK : (c + 1) * CHUNK * PACK],
+                )
+
+        z_hat = {}
+        moments = {}
+
+        def take_moments(ch):
+            for tt in chunk_tiles(ch):
+                stats = small.tile([P, H // BN_WIDTH, 6], F32)
+                for a in range(H // BN_WIDTH):
+                    nc.vector.bn_stats(out=stats[:, a, :], in_=z_all[:, tt, a * BN_WIDTH : (a + 1) * BN_WIDTH])
+                mean_var = small.tile([P, 2], F32)
+                nc.vector.bn_aggr(out=mean_var[:], in_=stats[:].rearrange("p a s -> p (a s)"))
+                var_eps = small.tile([P, 1], F32)
+                nc.gpsimd.tensor_scalar(
+                    out=var_eps[:], in0=mean_var[:, 1:2], scalar1=1.0, scalar2=LN_EPS, op0=ALU.mult, op1=ALU.add
+                )
+                rstd = small.tile([P, 1], F32)
+                nc.gpsimd.tensor_tensor(out=rstd[:], in0=var_eps[:], in1=neg_half[:], op=ALU.pow)
+                moments[tt] = (mean_var, rstd)
+
+        def normalise(ch):
+            for tt in chunk_tiles(ch):
+                mean_var, rstd = moments[tt]
+                zh = normed.tile([P, H], F32, name="zh")
+                nc.vector.tensor_scalar(
+                    out=zh[:], in0=z_all[:, tt, :], scalar1=mean_var[:, 0:1], scalar2=rstd[:],
+                    op0=ALU.subtract, op1=ALU.mult,
+                )
+                z_hat[tt] = zh
+
+        zn_tiles = {}
+
+        def transpose_normed(ch):
+            for c2 in range(PASSES):
+                zn = units.tile([P, PACK, CHUNK], F32)
+                for pair in range(PACK // 2):
+                    zt = psum.tile([P, 2, CHUNK], F32, tag="bank")
+                    for i in range(2):
+                        ft = c2 * PACK + pair * 2 + i
+                        for tl, tt in enumerate(chunk_tiles(ch)):
+                            nc.tensor.transpose(
+                                zt[:, i, tl * P : (tl + 1) * P], z_hat[tt][:, ft * P : (ft + 1) * P], ident_f32[:]
+                            )
+                    for i in range(2):
+                        ft = c2 * PACK + pair * 2 + i
+                        nc.scalar.activation(
+                            out=zn[:, pair * 2 + i, :],
+                            in_=zt[:, i, :],
+                            func=ACT.Identity,
+                            scale=gb_col[:, ft : ft + 1],
+                            bias=gb_col[:, FEATURE_TILES + ft : FEATURE_TILES + ft + 1],
+                        )
+                zn_tiles[(ch, c2)] = zn
+
+        silu_tiles = {}
+
+        def gate_matmul(ch):
+            for c2 in range(PASSES):
+                silu_g = units.tile([P, CHUNK, PACK], F32)
+                for tl, tt in enumerate(chunk_tiles(ch)):
+                    g_bank = psum.tile([P, PACK, P], F32, tag="bank")
+                    for j in range(PACK):
+                        ft = c2 * PACK + j
+                        for c in range(PASSES):
+                            nc.tensor.matmul_mx(
+                                out=g_bank[:, j, :],
+                                lhsT=wg_codes[:, c, ft * P : (ft + 1) * P].bitcast(FP8X4),
+                                lhsT_scale=wg_scales[:, c, ft * P : (ft + 1) * P],
+                                rhs=x_codes[:, c, tt * P : (tt + 1) * P].bitcast(FP8X4),
+                                rhs_scale=x_scales[:, c, tt * P : (tt + 1) * P],
+                                start=(c == 0),
+                                stop=(c == PASSES - 1),
+                            )
+                    nc.scalar.activation(
+                        out=silu_g[:, tl * P : (tl + 1) * P, :],
+                        in_=g_bank[:].rearrange("p j t -> p t j"),
+                        func=ACT.Silu,
+                    )
+                silu_tiles[(ch, c2)] = silu_g
+
+        def gate_product(ch, c2):
+            toks = slice(ch * CHUNK, (ch + 1) * CHUNK)
+            h_grouped = stage.tile([P, CHUNK, PACK], BF16, align_bytes=64)
+            nc.vector.tensor_tensor(
+                out=h_grouped[:],
+                in0=zn_tiles[(ch, c2)][:].rearrange("p j t -> p t j"),
+                in1=silu_tiles[(ch, c2)][:],
+                op=ALU.mult,
+            )
+            nc.vector.quantize_mx(
+                out=h_codes[:, c2, toks].bitcast(FP8X4),
+                scales=h_scales[:, c2, toks],
+                in_=h_grouped[:].rearrange("p t j -> p (t j)"),
+            )
+
+        o_banks = {}
+
+        def project_pass(ch, c2):
+            for tt in chunk_tiles(ch):
+                for first in range(0, H, N_OUT):
+                    if c2 == 0:
+                        o_banks[(tt, first)] = psum.tile([P, N_OUT], F32, tag="bank", name="o_bank")
+                    o_bank = o_banks[(tt, first)]
+                    nc.tensor.matmul_mx(
+                        out=o_bank[:],
+                        lhsT=h_codes[:, c2, tt * P : (tt + 1) * P].bitcast(FP8X4),
+                        lhsT_scale=h_scales[:, c2, tt * P : (tt + 1) * P],
+                        rhs=wo_codes[:, c2, first : first + N_OUT].bitcast(FP8X4),
+                        rhs_scale=wo_scales[:, c2, first : first + N_OUT],
+                        start=(c2 == 0),
+                        stop=(c2 == PASSES - 1),
+                    )
+                    if c2 == PASSES - 1:
+                        o_sb = result.tile([P, N_OUT], F32)
+                        nc.scalar.copy(out=o_sb[:], in_=o_bank[:])
+                        nc.sync.dma_start(out=out_dram[tt * P : (tt + 1) * P, first : first + N_OUT], in_=o_sb[:])
+
+        take_moments(0)
+        spread_gamma_beta()
+        transpose_x(0)
+        for ch in range(CHUNKS):
+            if ch + 1 < CHUNKS:
+                take_moments(ch + 1)
+                transpose_x(ch + 1)
+            normalise(ch)
+            transpose_normed(ch)
+            quantise_x(ch)
+        quantise_weight(wg_raw, wg_codes, wg_scales)
+        for ch in range(CHUNKS):
+            gate_matmul(ch)
+        quantise_weight(wo_raw, wo_codes, wo_scales)
+        for ch in range(CHUNKS):
+            for c2 in range(PASSES):
+                gate_product(ch, c2)
+                project_pass(ch, c2)

@@ -217,36 +217,33 @@ def tile_gatedlinearattention_pb_kernel(tc, z, hidden_states, Wg, Wo, gamma, bet
         silu_tiles = {}
 
         def gate_matmul(ch):
+            toks = slice(ch * CHUNK, (ch + 1) * CHUNK)
             for c2 in range(PASSES):
-                silu_g = units.tile([P, CHUNK, PACK], F32)
-                for tl, tt in enumerate(chunk_tiles(ch)):
-                    g_bank = psum.tile([P, PACK, P], F32, tag="bank")
-                    for j in range(PACK):
-                        ft = c2 * PACK + j
+                silu_g = units.tile([P, PACK, CHUNK], F32)
+                for pair in range(PACK // 2):
+                    g_bank = psum.tile([P, 2, CHUNK], F32, tag="bank")
+                    for i in range(2):
+                        ft = c2 * PACK + pair * 2 + i
                         for c in range(PASSES):
                             nc.tensor.matmul_mx(
-                                out=g_bank[:, j, :],
+                                out=g_bank[:, i, :],
                                 lhsT=wg_codes[:, c, ft * P : (ft + 1) * P].bitcast(FP8X4),
                                 lhsT_scale=wg_scales[:, c, ft * P : (ft + 1) * P],
-                                rhs=x_codes[:, c, tt * P : (tt + 1) * P].bitcast(FP8X4),
-                                rhs_scale=x_scales[:, c, tt * P : (tt + 1) * P],
+                                rhs=x_codes[:, c, toks].bitcast(FP8X4),
+                                rhs_scale=x_scales[:, c, toks],
                                 start=(c == 0),
                                 stop=(c == PASSES - 1),
                             )
-                    nc.scalar.activation(
-                        out=silu_g[:, tl * P : (tl + 1) * P, :],
-                        in_=g_bank[:].rearrange("p j t -> p t j"),
-                        func=ACT.Silu,
-                    )
+                    nc.scalar.activation(out=silu_g[:, pair * 2 : pair * 2 + 2, :], in_=g_bank[:], func=ACT.Silu)
                 silu_tiles[(ch, c2)] = silu_g
 
         def gate_product(ch, c2):
             toks = slice(ch * CHUNK, (ch + 1) * CHUNK)
             h_grouped = stage.tile([P, CHUNK, PACK], BF16, align_bytes=64)
             nc.vector.tensor_tensor(
-                out=h_grouped[:],
-                in0=zn_tiles[(ch, c2)][:].rearrange("p j t -> p t j"),
-                in1=silu_tiles[(ch, c2)][:],
+                out=h_grouped[:].rearrange("p (a i) j -> p a j i", i=4),
+                in0=zn_tiles[(ch, c2)][:].rearrange("p j (a i) -> p a j i", i=4),
+                in1=silu_tiles[(ch, c2)][:].rearrange("p j (a i) -> p a j i", i=4),
                 op=ALU.mult,
             )
             nc.vector.quantize_mx(

@@ -90,7 +90,7 @@ def tile_gatedlinearattention_pb_kernel(tc, z, hidden_states, Wg, Wo, gamma, bet
                 in_=Wo[c * K_PASS : (c + 1) * K_PASS, :].rearrange("(j p) m -> p j m", p=P),
             )
 
-        neg_half = keep.tile([P, 1], F32)
+        neg_half = keep.tile([P, CHUNK_TILES], F32)
         nc.gpsimd.memset(neg_half[:], -0.5)
         ident_f32 = keep.tile([P, P], F32)
         make_identity(nc, ident_f32[:])
@@ -163,29 +163,35 @@ def tile_gatedlinearattention_pb_kernel(tc, z, hidden_states, Wg, Wo, gamma, bet
                 )
 
         z_hat = {}
+        stats_tiles = {}
         moments = {}
 
-        def take_moments(ch):
-            for tt in chunk_tiles(ch):
-                stats = small.tile([P, H // BN_WIDTH, 6], F32)
+        def take_stats(ch):
+            stats = small.tile([P, CHUNK_TILES, H // BN_WIDTH, 6], F32)
+            for tl, tt in enumerate(chunk_tiles(ch)):
                 for a in range(H // BN_WIDTH):
-                    nc.vector.bn_stats(out=stats[:, a, :], in_=z_all[:, tt, a * BN_WIDTH : (a + 1) * BN_WIDTH])
-                mean_var = small.tile([P, 2], F32)
-                nc.vector.bn_aggr(out=mean_var[:], in_=stats[:].rearrange("p a s -> p (a s)"))
-                var_eps = small.tile([P, 1], F32)
-                nc.gpsimd.tensor_scalar(
-                    out=var_eps[:], in0=mean_var[:, 1:2], scalar1=1.0, scalar2=LN_EPS, op0=ALU.mult, op1=ALU.add
-                )
-                rstd = small.tile([P, 1], F32)
-                nc.gpsimd.tensor_tensor(out=rstd[:], in0=var_eps[:], in1=neg_half[:], op=ALU.pow)
-                moments[tt] = (mean_var, rstd)
+                    nc.vector.bn_stats(out=stats[:, tl, a, :], in_=z_all[:, tt, a * BN_WIDTH : (a + 1) * BN_WIDTH])
+            stats_tiles[ch] = stats
+
+        def aggregate(ch):
+            stats = stats_tiles[ch]
+            mean_var = small.tile([P, CHUNK_TILES, 2], F32)
+            for tl in range(CHUNK_TILES):
+                nc.vector.bn_aggr(out=mean_var[:, tl, :], in_=stats[:, tl].rearrange("p a s -> p (a s)"))
+            var_eps = small.tile([P, CHUNK_TILES], F32)
+            nc.gpsimd.tensor_scalar(
+                out=var_eps[:], in0=mean_var[:, :, 1], scalar1=1.0, scalar2=LN_EPS, op0=ALU.mult, op1=ALU.add
+            )
+            rstd = small.tile([P, CHUNK_TILES], F32)
+            nc.gpsimd.tensor_tensor(out=rstd[:], in0=var_eps[:], in1=neg_half[:], op=ALU.pow)
+            moments[ch] = (mean_var, rstd)
 
         def normalise(ch):
-            for tt in chunk_tiles(ch):
-                mean_var, rstd = moments[tt]
+            mean_var, rstd = moments[ch]
+            for tl, tt in enumerate(chunk_tiles(ch)):
                 zh = normed.tile([P, H], F32, name="zh")
                 nc.vector.tensor_scalar(
-                    out=zh[:], in0=z_all[:, tt, :], scalar1=mean_var[:, 0:1], scalar2=rstd[:],
+                    out=zh[:], in0=z_all[:, tt, :], scalar1=mean_var[:, tl, 0:1], scalar2=rstd[:, tl : tl + 1],
                     op0=ALU.subtract, op1=ALU.mult,
                 )
                 z_hat[tt] = zh
@@ -237,8 +243,9 @@ def tile_gatedlinearattention_pb_kernel(tc, z, hidden_states, Wg, Wo, gamma, bet
                     nc.scalar.activation(out=silu_g[:, pair * 2 : pair * 2 + 2, :], in_=g_bank[:], func=ACT.Silu)
                 silu_tiles[(ch, c2)] = silu_g
 
+        h_tiles = {}
+
         def gate_product(ch, c2):
-            toks = slice(ch * CHUNK, (ch + 1) * CHUNK)
             h_grouped = stage.tile([P, CHUNK, PACK], BF16, align_bytes=64)
             nc.vector.tensor_tensor(
                 out=h_grouped[:].rearrange("p (a i) j -> p a j i", i=4),
@@ -246,10 +253,14 @@ def tile_gatedlinearattention_pb_kernel(tc, z, hidden_states, Wg, Wo, gamma, bet
                 in1=silu_tiles[(ch, c2)][:].rearrange("p j (a i) -> p a j i", i=4),
                 op=ALU.mult,
             )
+            h_tiles[(ch, c2)] = h_grouped
+
+        def quantise_h(ch, c2):
+            toks = slice(ch * CHUNK, (ch + 1) * CHUNK)
             nc.vector.quantize_mx(
                 out=h_codes[:, c2, toks].bitcast(FP8X4),
                 scales=h_scales[:, c2, toks],
-                in_=h_grouped[:].rearrange("p t j -> p (t j)"),
+                in_=h_tiles[(ch, c2)][:].rearrange("p t j -> p (t j)"),
             )
 
         o_banks = {}
@@ -274,21 +285,30 @@ def tile_gatedlinearattention_pb_kernel(tc, z, hidden_states, Wg, Wo, gamma, bet
                         nc.scalar.copy(out=o_sb[:], in_=o_bank[:])
                         nc.sync.dma_start(out=out_dram[tt * P : (tt + 1) * P, first : first + N_OUT], in_=o_sb[:])
 
-        take_moments(0)
+        take_stats(0)
         spread_gamma_beta()
+        aggregate(0)
         transpose_x(0)
         for ch in range(CHUNKS):
             if ch + 1 < CHUNKS:
-                take_moments(ch + 1)
+                take_stats(ch + 1)
                 transpose_x(ch + 1)
+            quantise_x(ch)
+            if ch + 1 < CHUNKS:
+                aggregate(ch + 1)
             normalise(ch)
             transpose_normed(ch)
-            quantise_x(ch)
         quantise_weight(wg_raw, wg_codes, wg_scales)
         for ch in range(CHUNKS):
             gate_matmul(ch)
         quantise_weight(wo_raw, wo_codes, wo_scales)
+        waiting = None
         for ch in range(CHUNKS):
             for c2 in range(PASSES):
                 gate_product(ch, c2)
-                project_pass(ch, c2)
+                if waiting is not None:
+                    quantise_h(waiting[0], waiting[1])
+                    project_pass(waiting[0], waiting[1])
+                waiting = (ch, c2)
+        quantise_h(waiting[0], waiting[1])
+        project_pass(waiting[0], waiting[1])

@@ -92,6 +92,8 @@ def tile_gatedlinearattention_pb_kernel(tc, z, hidden_states, Wg, Wo, gamma, bet
 
         neg_half = keep.tile([P, CHUNK_TILES], F32)
         nc.gpsimd.memset(neg_half[:], -0.5)
+        table_warmer = keep.tile([P, 1], F32)
+        nc.scalar.activation(out=table_warmer[:], in_=neg_half[:, 0:1], func=ACT.Silu)
         ident_f32 = keep.tile([P, P], F32)
         make_identity(nc, ident_f32[:])
         ident_bf16 = keep.tile([P, P], BF16)
@@ -120,19 +122,18 @@ def tile_gatedlinearattention_pb_kernel(tc, z, hidden_states, Wg, Wo, gamma, bet
                 in_=grouped[:].rearrange("p n j -> p (n j)"),
             )
 
-        def quantise_weight(raw, codes, scales):
+        def quantise_weight(raw, codes, scales, pieces):
             waiting = None
-            for c in range(PASSES):
-                for first in range(0, H, W_PIECE):
-                    cols = slice(first, first + W_PIECE)
-                    grouped = stage.tile([P, W_PIECE, PACK], BF16, align_bytes=64)
-                    nc.vector.tensor_copy(
-                        out=grouped[:].rearrange("p (a i) j -> p a j i", i=4),
-                        in_=raw[:, c, :, cols].rearrange("p j (a i) -> p a j i", i=4),
-                    )
-                    if waiting is not None:
-                        quantise_piece(waiting, codes, scales)
-                    waiting = (grouped, c, cols)
+            for c, first in pieces:
+                cols = slice(first, first + W_PIECE)
+                grouped = stage.tile([P, W_PIECE, PACK], BF16, align_bytes=64)
+                nc.vector.tensor_copy(
+                    out=grouped[:].rearrange("p (a i) j -> p a j i", i=4),
+                    in_=raw[:, c, :, cols].rearrange("p j (a i) -> p a j i", i=4),
+                )
+                if waiting is not None:
+                    quantise_piece(waiting, codes, scales)
+                waiting = (grouped, c, cols)
             quantise_piece(waiting, codes, scales)
 
         x_words = x_all[:].bitcast(F32)
@@ -222,26 +223,25 @@ def tile_gatedlinearattention_pb_kernel(tc, z, hidden_states, Wg, Wo, gamma, bet
 
         silu_tiles = {}
 
-        def gate_matmul(ch):
+        def gate_matmul(ch, c2):
             toks = slice(ch * CHUNK, (ch + 1) * CHUNK)
-            for c2 in range(PASSES):
-                silu_g = units.tile([P, PACK, CHUNK], F32)
-                for pair in range(PACK // 2):
-                    g_bank = psum.tile([P, 2, CHUNK], F32, tag="bank")
-                    for i in range(2):
-                        ft = c2 * PACK + pair * 2 + i
-                        for c in range(PASSES):
-                            nc.tensor.matmul_mx(
-                                out=g_bank[:, i, :],
-                                lhsT=wg_codes[:, c, ft * P : (ft + 1) * P].bitcast(FP8X4),
-                                lhsT_scale=wg_scales[:, c, ft * P : (ft + 1) * P],
-                                rhs=x_codes[:, c, toks].bitcast(FP8X4),
-                                rhs_scale=x_scales[:, c, toks],
-                                start=(c == 0),
-                                stop=(c == PASSES - 1),
-                            )
-                    nc.scalar.activation(out=silu_g[:, pair * 2 : pair * 2 + 2, :], in_=g_bank[:], func=ACT.Silu)
-                silu_tiles[(ch, c2)] = silu_g
+            silu_g = units.tile([P, PACK, CHUNK], F32)
+            for pair in range(PACK // 2):
+                g_bank = psum.tile([P, 2, CHUNK], F32, tag="bank")
+                for i in range(2):
+                    ft = c2 * PACK + pair * 2 + i
+                    for c in range(PASSES):
+                        nc.tensor.matmul_mx(
+                            out=g_bank[:, i, :],
+                            lhsT=wg_codes[:, c, ft * P : (ft + 1) * P].bitcast(FP8X4),
+                            lhsT_scale=wg_scales[:, c, ft * P : (ft + 1) * P],
+                            rhs=x_codes[:, c, toks].bitcast(FP8X4),
+                            rhs_scale=x_scales[:, c, toks],
+                            start=(c == 0),
+                            stop=(c == PASSES - 1),
+                        )
+                nc.scalar.activation(out=silu_g[:, pair * 2 : pair * 2 + 2, :], in_=g_bank[:], func=ACT.Silu)
+            silu_tiles[(ch, c2)] = silu_g
 
         h_tiles = {}
 
@@ -298,10 +298,15 @@ def tile_gatedlinearattention_pb_kernel(tc, z, hidden_states, Wg, Wo, gamma, bet
                 aggregate(ch + 1)
             normalise(ch)
             transpose_normed(ch)
-        quantise_weight(wg_raw, wg_codes, wg_scales)
-        for ch in range(CHUNKS):
-            gate_matmul(ch)
-        quantise_weight(wo_raw, wo_codes, wo_scales)
+        quantise_weight(
+            wg_raw, wg_codes, wg_scales, [(c, first) for first in range(0, H, W_PIECE) for c in range(PASSES)]
+        )
+        for c2 in range(PASSES):
+            for ch in range(CHUNKS):
+                gate_matmul(ch, c2)
+        quantise_weight(
+            wo_raw, wo_codes, wo_scales, [(c, first) for c in range(PASSES) for first in range(0, H, W_PIECE)]
+        )
         waiting = None
         for ch in range(CHUNKS):
             for c2 in range(PASSES):

from contextlib import ExitStack

import concourse.mybir as mybir
from concourse.masks import make_identity

F32 = mybir.dt.float32
BF16 = mybir.dt.bfloat16
U32 = mybir.dt.uint32
U8 = mybir.dt.uint8
FP8X4 = mybir.dt.float8_e4m3fn_x4
ALU = mybir.AluOpType
ACT = mybir.ActivationFunctionType

P = 128
PACK = 4
K_PASS = P * PACK
TOKENS = 1024
H = 1024
PASSES = H // K_PASS
TOKEN_TILES = TOKENS // P
FEATURE_TILES = H // P
CHUNK_TILES = 2
CHUNK = CHUNK_TILES * P
CHUNKS = TOKENS // CHUNK
N_OUT = 512
LN_EPS = 1e-5
W_PIECE = 512
BN_WIDTH = 512

FLOPS = 2 * 2 * TOKENS * H * H


def tile_gatedlinearattention_pb_kernel(tc, z, hidden_states, Wg, Wo, gamma, beta, out):
    nc = tc.nc
    x_dram = hidden_states.flatten_outer_dims()
    z_dram = z.flatten_outer_dims()
    out_dram = out.flatten_outer_dims()

    with ExitStack() as ctx:
        ctx.enter_context(tc.manual_schedule())
        keep = ctx.enter_context(tc.tile_pool(name="keep", bufs=1))
        stage = ctx.enter_context(tc.tile_pool(name="stage", bufs=3))
        small = ctx.enter_context(tc.tile_pool(name="small", bufs=TOKEN_TILES))
        normed = ctx.enter_context(tc.tile_pool(name="normed", bufs=2 * CHUNK_TILES))
        units = ctx.enter_context(tc.tile_pool(name="units", bufs=CHUNKS * PASSES))
        result = ctx.enter_context(tc.tile_pool(name="result", bufs=6))
        psum = ctx.enter_context(tc.psum_pool(name="psum", bufs=8))

        def chunk_tiles(ch):
            return range(ch * CHUNK_TILES, (ch + 1) * CHUNK_TILES)

        z_all = keep.tile([P, TOKEN_TILES, H], BF16)
        x_all = keep.tile([P, TOKEN_TILES * H], BF16)
        wg_raw = keep.tile([P, PASSES, PACK, H], BF16)
        wo_raw = keep.tile([P, PASSES, PACK, H], BF16)

        def load_z(ch):
            first = ch * CHUNK_TILES
            nc.sync.dma_start(
                out=z_all[:, first : first + CHUNK_TILES, :],
                in_=z_dram[ch * CHUNK : (ch + 1) * CHUNK, :].rearrange("(t p) k -> p t k", p=P),
            )

        def load_x(ch):
            nc.sync.dma_start(
                out=x_all[:, ch * CHUNK_TILES * H : (ch + 1) * CHUNK_TILES * H].rearrange("p (t k) -> p t k", k=H),
                in_=x_dram[ch * CHUNK : (ch + 1) * CHUNK, :].rearrange("(t p) k -> p t k", p=P),
            )

        gb_rows = keep.tile([P, P], BF16)
        nc.gpsimd.memset(gb_rows[:], 0.0)

        load_z(0)
        nc.sync.dma_start(out=gb_rows[0:FEATURE_TILES, :], in_=gamma.rearrange("(f p) -> f p", p=P))
        nc.sync.dma_start(
            out=gb_rows[FEATURE_TILES : 2 * FEATURE_TILES, :], in_=beta.rearrange("(f p) -> f p", p=P)
        )
        load_x(0)
        for ch in range(1, CHUNKS):
            load_z(ch)
            load_x(ch)
        for c in range(PASSES):
            nc.sync.dma_start(
                out=wg_raw[:, c].rearrange("q (u e) n -> q u e n", u=2),
                in_=Wg[c * K_PASS : (c + 1) * K_PASS, :].rearrange("(u q e) n -> q u e n", u=2, e=2),
            )
        for c in range(PASSES):
            nc.sync.dma_start(
                out=wo_raw[:, c],
                in_=Wo[c * K_PASS : (c + 1) * K_PASS, :].rearrange("(j p) m -> p j m", p=P),
            )

        neg_half = keep.tile([P, CHUNK_TILES], F32)
        nc.gpsimd.memset(neg_half[:], -0.5)
        table_warmer = keep.tile([P, 1], F32)
        nc.scalar.activation(out=table_warmer[:], in_=neg_half[:, 0:1], func=ACT.Silu)
        ident_f32 = keep.tile([P, P], F32)
        make_identity(nc, ident_f32[:])
        ident_bf16 = keep.tile([P, P], BF16)
        make_identity(nc, ident_bf16[:])
        gb_col = keep.tile([P, 2 * FEATURE_TILES], F32)

        def spread_gamma_beta():
            gb_t = psum.tile([P, P], BF16, tag="bank")
            nc.tensor.transpose(gb_t[:], gb_rows[:], ident_bf16[:])
            nc.vector.tensor_copy(out=gb_col[:], in_=gb_t[:, 0 : 2 * FEATURE_TILES])

        wg_codes = keep.tile([P, PASSES, H], U32, align_bytes=64)
        wg_scales = keep.tile([P, PASSES, H], U8, align_bytes=64)
        wo_codes = keep.tile([P, PASSES, H], U32, align_bytes=64)
        wo_scales = keep.tile([P, PASSES, H], U8, align_bytes=64)
        x_codes = keep.tile([P, PASSES, TOKENS], U32, align_bytes=64)
        x_scales = keep.tile([P, PASSES, TOKENS], U8, align_bytes=64)
        h_codes = keep.tile([P, PASSES, TOKENS], U32, align_bytes=64)
        h_scales = keep.tile([P, PASSES, TOKENS], U8, align_bytes=64)

        def quantise_piece(piece, codes, scales):
            grouped, c, cols = piece
            nc.vector.quantize_mx(
                out=codes[:, c, cols].bitcast(FP8X4),
                scales=scales[:, c, cols],
                in_=grouped[:].rearrange("p n j -> p (n j)"),
            )

        def quantise_weight(raw, codes, scales, pieces):
            waiting = None
            for c, first in pieces:
                cols = slice(first, first + W_PIECE)
                grouped = stage.tile([P, W_PIECE, PACK], BF16, align_bytes=64)
                nc.vector.tensor_copy(
                    out=grouped[:].rearrange("p (a i) j -> p a j i", i=4),
                    in_=raw[:, c, :, cols].rearrange("p j (a i) -> p a j i", i=4),
                )
                if waiting is not None:
                    quantise_piece(waiting, codes, scales)
                waiting = (grouped, c, cols)
            quantise_piece(waiting, codes, scales)

        x_words = x_all[:].bitcast(F32)
        words_per_tile = H // 2
        x_grouped = {}

        def transpose_x(ch):
            grouped = stage.tile([P, PASSES * CHUNK * PACK], BF16, align_bytes=64, name="x_grouped")
            grouped_words = grouped[:].bitcast(F32).rearrange("p (c t u) -> p c t u", c=PASSES, u=2)
            for tl, tt in enumerate(chunk_tiles(ch)):
                xt = psum.tile([P, 2 * PASSES, P], F32, tag="bank")
                for b in range(2 * PASSES):
                    first = tt * words_per_tile + b * P
                    nc.tensor.transpose(xt[:, b, :], x_words[:, first : first + P], ident_f32[:])
                nc.scalar.copy(
                    out=grouped_words[:, :, tl * P : (tl + 1) * P, :],
                    in_=xt[:].rearrange("p (c u) t -> p c t u", u=2),
                )
            x_grouped[ch] = grouped

        def quantise_x(ch):
            toks = slice(ch * CHUNK, (ch + 1) * CHUNK)
            for c in range(PASSES):
                nc.vector.quantize_mx(
                    out=x_codes[:, c, toks].bitcast(FP8X4),
                    scales=x_scales[:, c, toks],
                    in_=x_grouped[ch][:, c * CHUNK * PACK : (c + 1) * CHUNK * PACK],
                )

        z_hat = {}
        stats_tiles = {}
        moments = {}

        def take_stats(ch):
            stats = small.tile([P, CHUNK_TILES, H // BN_WIDTH, 6], F32)
            for tl, tt in enumerate(chunk_tiles(ch)):
                for a in range(H // BN_WIDTH):
                    nc.vector.bn_stats(out=stats[:, tl, a, :], in_=z_all[:, tt, a * BN_WIDTH : (a + 1) * BN_WIDTH])
            stats_tiles[ch] = stats

        def aggregate(ch):
            stats = stats_tiles[ch]
            mean_var = small.tile([P, CHUNK_TILES, 2], F32)
            for tl in range(CHUNK_TILES):
                nc.vector.bn_aggr(out=mean_var[:, tl, :], in_=stats[:, tl].rearrange("p a s -> p (a s)"))
            var_eps = small.tile([P, CHUNK_TILES], F32)
            nc.gpsimd.tensor_scalar(
                out=var_eps[:], in0=mean_var[:, :, 1], scalar1=1.0, scalar2=LN_EPS, op0=ALU.mult, op1=ALU.add
            )
            rstd = small.tile([P, CHUNK_TILES], F32)
            nc.gpsimd.tensor_tensor(out=rstd[:], in0=var_eps[:], in1=neg_half[:], op=ALU.pow)
            moments[ch] = (mean_var, rstd)

        def normalise(ch):
            mean_var, rstd = moments[ch]
            for tl, tt in enumerate(chunk_tiles(ch)):
                zh = normed.tile([P, H], F32, name="zh")
                nc.vector.tensor_scalar(
                    out=zh[:], in0=z_all[:, tt, :], scalar1=mean_var[:, tl, 0:1], scalar2=rstd[:, tl : tl + 1],
                    op0=ALU.subtract, op1=ALU.mult,
                )
                z_hat[tt] = zh

        zn_tiles = {}

        def transpose_normed(ch):
            for c2 in range(PASSES):
                zn = units.tile([P, PACK, CHUNK], F32)
                for pair in range(PACK // 2):
                    zt = psum.tile([P, 2, CHUNK], F32, tag="bank")
                    for i in range(2):
                        ft = c2 * PACK + pair * 2 + i
                        for tl, tt in enumerate(chunk_tiles(ch)):
                            nc.tensor.transpose(
                                zt[:, i, tl * P : (tl + 1) * P], z_hat[tt][:, ft * P : (ft + 1) * P], ident_f32[:]
                            )
                    for i in range(2):
                        ft = c2 * PACK + pair * 2 + i
                        nc.scalar.activation(
                            out=zn[:, pair * 2 + i, :],
                            in_=zt[:, i, :],
                            func=ACT.Identity,
                            scale=gb_col[:, ft : ft + 1],
                            bias=gb_col[:, FEATURE_TILES + ft : FEATURE_TILES + ft + 1],
                        )
                zn_tiles[(ch, c2)] = zn

        silu_tiles = {}

        def gate_matmul(ch, c2):
            toks = slice(ch * CHUNK, (ch + 1) * CHUNK)
            silu_g = units.tile([P, PACK, CHUNK], F32)
            for pair in range(PACK // 2):
                g_bank = psum.tile([P, 2, CHUNK], F32, tag="bank")
                for i in range(2):
                    ft = c2 * PACK + pair * 2 + i
                    for c in range(PASSES):
                        nc.tensor.matmul_mx(
                            out=g_bank[:, i, :],
                            lhsT=wg_codes[:, c, ft * P : (ft + 1) * P].bitcast(FP8X4),
                            lhsT_scale=wg_scales[:, c, ft * P : (ft + 1) * P],
                            rhs=x_codes[:, c, toks].bitcast(FP8X4),
                            rhs_scale=x_scales[:, c, toks],
                            start=(c == 0),
                            stop=(c == PASSES - 1),
                        )
                nc.scalar.activation(out=silu_g[:, pair * 2 : pair * 2 + 2, :], in_=g_bank[:], func=ACT.Silu)
            silu_tiles[(ch, c2)] = silu_g

        h_tiles = {}

        def gate_product(ch, c2):
            h_grouped = stage.tile([P, CHUNK, PACK], BF16, align_bytes=64)
            nc.vector.tensor_tensor(
                out=h_grouped[:].rearrange("p (a i) j -> p a j i", i=4),
                in0=zn_tiles[(ch, c2)][:].rearrange("p j (a i) -> p a j i", i=4),
                in1=silu_tiles[(ch, c2)][:].rearrange("p j (a i) -> p a j i", i=4),
                op=ALU.mult,
            )
            h_tiles[(ch, c2)] = h_grouped

        def quantise_h(ch, c2):
            toks = slice(ch * CHUNK, (ch + 1) * CHUNK)
            nc.vector.quantize_mx(
                out=h_codes[:, c2, toks].bitcast(FP8X4),
                scales=h_scales[:, c2, toks],
                in_=h_tiles[(ch, c2)][:].rearrange("p t j -> p (t j)"),
            )

        o_banks = {}

        def project_pass(ch, c2):
            for tt in chunk_tiles(ch):
                for first in range(0, H, N_OUT):
                    if c2 == 0:
                        o_banks[(tt, first)] = psum.tile([P, N_OUT], F32, tag="bank", name="o_bank")
                    o_bank = o_banks[(tt, first)]
                    nc.tensor.matmul_mx(
                        out=o_bank[:],
                        lhsT=h_codes[:, c2, tt * P : (tt + 1) * P].bitcast(FP8X4),
                        lhsT_scale=h_scales[:, c2, tt * P : (tt + 1) * P],
                        rhs=wo_codes[:, c2, first : first + N_OUT].bitcast(FP8X4),
                        rhs_scale=wo_scales[:, c2, first : first + N_OUT],
                        start=(c2 == 0),
                        stop=(c2 == PASSES - 1),
                    )
                    if c2 == PASSES - 1:
                        o_sb = result.tile([P, N_OUT], F32)
                        nc.scalar.copy(out=o_sb[:], in_=o_bank[:])
                        nc.sync.dma_start(out=out_dram[tt * P : (tt + 1) * P, first : first + N_OUT], in_=o_sb[:])

        take_stats(0)
        spread_gamma_beta()
        aggregate(0)
        transpose_x(0)
        for ch in range(CHUNKS):
            if ch + 1 < CHUNKS:
                take_stats(ch + 1)
                transpose_x(ch + 1)
            quantise_x(ch)
            if ch + 1 < CHUNKS:
                aggregate(ch + 1)
            normalise(ch)
            transpose_normed(ch)
        quantise_weight(
            wg_raw, wg_codes, wg_scales, [(c, first) for first in range(0, H, W_PIECE) for c in range(PASSES)]
        )
        for c2 in range(PASSES):
            for ch in range(CHUNKS):
                gate_matmul(ch, c2)
        quantise_weight(
            wo_raw, wo_codes, wo_scales, [(c, first) for c in range(PASSES) for first in range(0, H, W_PIECE)]
        )
        waiting = None
        for ch in range(CHUNKS):
            for c2 in range(PASSES):
                gate_product(ch, c2)
                if waiting is not None:
                    quantise_h(waiting[0], waiting[1])
                    project_pass(waiting[0], waiting[1])
                waiting = (ch, c2)
        quantise_h(waiting[0], waiting[1])
        project_pass(waiting[0], waiting[1])
